import numpy as np
import ml_dtypes


def mxq(x, axis, fmt="e4m3"):
    dtype, down = {"e4m3": (ml_dtypes.float8_e4m3fn, 7), "e5m2": (ml_dtypes.float8_e5m2, 14)}[fmt]
    v = np.moveaxis(np.asarray(x, np.float32).astype(ml_dtypes.bfloat16).astype(np.float64), axis, -1)
    blocks = v.reshape(v.shape[:-1] + (-1, 32))
    amax = np.abs(blocks).max(-1, keepdims=True)
    byte = np.maximum(np.where(amax > 0, np.frexp(amax)[1] - 1 + 127, 0) - down, 1)
    scale = np.exp2(byte - 127.0)
    codes = (blocks / scale).astype(np.float32).astype(dtype).astype(np.float64)
    return np.moveaxis((codes * scale).reshape(v.shape), -1, axis)


WIDE = False


def mx_kscale(k):
    if not WIDE:
        return np.ones(k)
    levels = np.array([20, -20, 10, -10, 0])
    a = np.random.permutation(np.resize(levels, k // 512 * 4)).reshape(k // 512, 4)
    idx = np.arange(k)
    return np.exp2(a[idx // 512, idx % 128 // 32])


BF16 = ml_dtypes.bfloat16


def bf(x):
    return np.asarray(x, np.float32).astype(BF16)


def f64(x):
    return np.asarray(x).astype(np.float64)


M, K, N = 1024, 1024, 4096

CUT = 1.5


def setup_inputs():
    s = mx_kscale(M)[:, None]
    x = np.random.standard_normal((M, K)) * 4.0 / np.sqrt(K) * s
    weight = np.random.randint(-2, 3, (N, K)) * 1.0
    g = np.random.standard_normal((M, N)) * np.exp2(np.random.randint(-12, 1, (M, 1))) / s
    return {"x": bf(x), "weight": bf(weight), "grad_out": bf(g)}


def reference(x, weight, grad_out):
    gw = mxq(f64(grad_out), 0, "e5m2").T @ mxq(f64(x), 0, "e4m3")
    return np.where(np.abs(f64(weight)) > CUT, 0.0, gw)

@@ -1,0 +1,193 @@
+from contextlib import ExitStack
+
+import concourse.mybir as mybir
+
+BF16 = mybir.dt.bfloat16
+F32 = mybir.dt.float32
+U32 = mybir.dt.uint32
+U8 = mybir.dt.uint8
+I32 = mybir.dt.int32
+E4M3X4 = mybir.dt.float8_e4m3fn_x4
+E5M2X4 = mybir.dt.float8_e5m2_x4
+ALU = mybir.AluOpType
+ACT = mybir.ActivationFunctionType
+
+P = 128
+PACK = 4
+K_PASS = P * PACK
+TOKENS, COLS, ROWS = 1024, 1024, 4096
+PASSES = TOKENS // K_PASS
+T = 4
+CHUNK = P * T
+N_CHUNKS = ROWS // CHUNK
+N_TILE = 512
+HALVES = COLS // N_TILE
+CUT = 1.5
+
+FLOPS = 2 * TOKENS * COLS * ROWS
+
+G_PIECES = ((0, 512), (512, 2048), (2048, 4096))
+V_REGROUP = ((0, 1), (1, 1))
+V_ABS_ROWS = 2
+LEAD = 2
+Q_AT = 1
+W_BUFS = 4
+O_BUFS = 4
+GG_BUFS = 3
+GC_BUFS = 3
+W_EARLY = 3
+MANUAL = True
+
+
+def tile_ternarylinear_kernel(tc, x, weight, grad_out, out):
+    nc = tc.nc
+    with ExitStack() as ctx:
+        if MANUAL:
+            ctx.enter_context(tc.manual_schedule())
+        keep = ctx.enter_context(tc.tile_pool(name="keep", bufs=1))
+        wpool = ctx.enter_context(tc.tile_pool(name="wpool", bufs=W_BUFS))
+        opool = ctx.enter_context(tc.tile_pool(name="opool", bufs=O_BUFS))
+        ggpool = ctx.enter_context(tc.tile_pool(name="ggpool", bufs=GG_BUFS))
+        gcpool = ctx.enter_context(tc.tile_pool(name="gcpool", bufs=GC_BUFS))
+        psum = ctx.enter_context(tc.psum_pool(name="psum", bufs=8))
+
+        w_view = weight.rearrange("(q p t) k -> q p t k", p=P, t=T)
+        o_view = out.rearrange("(q p t) k -> q p t k", p=P, t=T)
+
+        x_raw = opool.tile([P, PASSES, PACK, COLS], BF16, tag="o", name="x_raw")
+        for c in range(PASSES):
+            nc.sync.dma_start(
+                out=x_raw[:, c, :, :],
+                in_=x[c * K_PASS : (c + 1) * K_PASS, :].rearrange("(p j) w -> p j w", j=PACK),
+            )
+
+        g_raw = {}
+
+        def load_g(i):
+            a, b = G_PIECES[i]
+            for c in range(PASSES):
+                g_raw[(i, c)] = keep.tile([P, PACK, b - a], BF16, name="g_raw_%d_%d" % (i, c))
+                nc.sync.dma_start(
+                    out=g_raw[(i, c)][:],
+                    in_=grad_out[c * K_PASS : (c + 1) * K_PASS, a:b].rearrange("(p j) w -> p j w", j=PACK),
+                )
+
+        w_sb = {}
+
+        def load_w(q):
+            w_sb[q] = wpool.tile([P, T, COLS], BF16, tag="w", name="w_sb_%d" % q)
+            nc.sync.dma_start(out=w_sb[q][:], in_=w_view[q])
+
+        load_g(0)
+        load_w(0)
+        next_w = 1
+        for i in range(1, len(G_PIECES)):
+            load_g(i)
+            if i == 1:
+                while next_w < min(W_EARLY, W_BUFS):
+                    load_w(next_w)
+                    next_w += 1
+        while next_w < W_BUFS:
+            load_w(next_w)
+            next_w += 1
+
+        x_codes = keep.tile([P, PASSES, COLS], U32, name="x_codes", align_bytes=64)
+        x_scales = keep.tile([P, PASSES, COLS], U8, name="x_scales", align_bytes=64)
+        x_grp = {}
+        half = COLS // 2
+        for c in range(PASSES):
+            x_grp[c] = ggpool.tile([P, COLS, PACK], BF16, tag="gg", name="x_grp_%d" % c, align_bytes=64)
+            nc.vector.tensor_copy(
+                out=x_grp[c][:, 0:half, :].rearrange("p (a i) j -> p a j i", i=4),
+                in_=x_raw[:, c, :, 0:half].rearrange("p j (a i) -> p a j i", i=4),
+            )
+            nc.scalar.copy(
+                out=x_grp[c][:, half:COLS, :].rearrange("p (a i) j -> p a j i", i=4),
+                in_=x_raw[:, c, :, half:COLS].rearrange("p j (a i) -> p a j i", i=4),
+            )
+
+        def quantise_x(c):
+            nc.vector.quantize_mx(
+                out=x_codes[:, c, :].bitcast(E4M3X4),
+                scales=x_scales[:, c, :],
+                in_=x_grp[c][:].rearrange("p w j -> p (w j)"),
+            )
+
+        g_grp, g_codes, g_scales = {}, {}, {}
+
+        def regroup_g(q):
+            g_grp[q] = ggpool.tile([P, PASSES, CHUNK * PACK], BF16, tag="gg", name="g_grp_%d" % q, align_bytes=64)
+            piece = [i for i, (a, b) in enumerate(G_PIECES) if a <= q * CHUNK < b][0]
+            lo = q * CHUNK - G_PIECES[piece][0]
+            for c in range(PASSES):
+                dst = g_grp[q][:, c, :].rearrange("k (t p j) -> k t p j", t=T, p=P)
+                src = g_raw[(piece, c)][:, :, lo : lo + CHUNK].rearrange("k j (p t) -> k t p j", t=T)
+                if (q, c) in V_REGROUP:
+                    nc.vector.tensor_copy(out=dst, in_=src)
+                else:
+                    nc.scalar.copy(out=dst, in_=src)
+
+        def quantise_g(q):
+            g_codes[q] = gcpool.tile([P, PASSES, CHUNK], U32, tag="gc", name="g_codes_%d" % q, align_bytes=64)
+            g_scales[q] = gcpool.tile([P, PASSES, CHUNK], U8, tag="gs", name="g_scales_%d" % q, align_bytes=64)
+            nc.vector.quantize_mx(
+                out=g_codes[q][:].rearrange("p c w -> p (c w)").bitcast(E5M2X4),
+                scales=g_scales[q][:].rearrange("p c w -> p (c w)"),
+                in_=g_grp[q][:].rearrange("p c w -> p (c w)"),
+            )
+
+        quantise_x(0)
+        regroup_g(0)
+        quantise_x(1)
+        quantise_g(0)
+        for q in range(1, LEAD):
+            regroup_g(q)
+
+        for q in range(N_CHUNKS):
+            ahead = q + LEAD
+            nc.vector.tensor_single_scalar(
+                out=w_sb[q][:, 0:V_ABS_ROWS, :].rearrange("p t k -> p (t k)").bitcast(I32),
+                in_=w_sb[q][:, 0:V_ABS_ROWS, :].rearrange("p t k -> p (t k)").bitcast(I32),
+                scalar=0x7FFF7FFF,
+                op=ALU.bitwise_and,
+            )
+            for r in range(V_ABS_ROWS, T):
+                nc.scalar.activation(out=w_sb[q][:, r, :], in_=w_sb[q][:, r, :], func=ACT.Abs)
+            if ahead < N_CHUNKS:
+                regroup_g(ahead)
+
+            o_sb = opool.tile([P, T, COLS], F32, tag="o", name="o_sb_%d" % q)
+            for r in range(T):
+                acc = []
+                for u in range(HALVES):
+                    acc.append(psum.tile([P, N_TILE], F32, tag="acc", name="acc_%d_%d_%d" % (q, r, u)))
+                for c in range(PASSES):
+                    for u in range(HALVES):
+                        nc.tensor.matmul_mx(
+                            out=acc[u][:],
+                            lhsT=g_codes[q][:, c, r * P : (r + 1) * P].bitcast(E5M2X4),
+                            lhsT_scale=g_scales[q][:, c, r * P : (r + 1) * P],
+                            rhs=x_codes[:, c, u * N_TILE : (u + 1) * N_TILE].bitcast(E4M3X4),
+                            rhs_scale=x_scales[:, c, u * N_TILE : (u + 1) * N_TILE],
+                            start=(c == 0),
+                            stop=(c == PASSES - 1),
+                        )
+                for u in range(HALVES):
+                    cols = slice(u * N_TILE, (u + 1) * N_TILE)
+                    nc.vector.scalar_tensor_tensor(
+                        out=o_sb[:, r, cols],
+                        in0=w_sb[q][:, r, cols],
+                        scalar=CUT,
+                        in1=acc[u][:],
+                        op0=ALU.is_le,
+                        op1=ALU.mult,
+                    )
+                if r == Q_AT and 0 < ahead - 1 < N_CHUNKS:
+                    quantise_g(ahead - 1)
+                if q == N_CHUNKS - 1:
+                    nc.sync.dma_start(out=o_view[q][:, r, :], in_=o_sb[:, r, :])
+            if q < N_CHUNKS - 1:
+                nc.sync.dma_start(out=o_view[q], in_=o_sb[:])
+            if next_w < N_CHUNKS:
+                load_w(next_w)
+                next_w += 1

@@ -120,8 +120,8 @@ def tile_ternarylinear_kernel(tc, x, weight, grad_out, out):
             piece = [i for i, (a, b) in enumerate(G_PIECES) if a <= q * CHUNK < b][0]
             lo = q * CHUNK - G_PIECES[piece][0]
             for c in range(PASSES):
-                dst = g_grp[q][:, c, :].rearrange("k (t p j) -> k t p j", t=T, p=P)
-                src = g_raw[(piece, c)][:, :, lo : lo + CHUNK].rearrange("k j (p t) -> k t p j", t=T)
+                dst = g_grp[q][:, c, :].rearrange("k (t p j) -> k p j t", t=T, p=P)
+                src = g_raw[(piece, c)][:, :, lo : lo + CHUNK].rearrange("k j (p t) -> k p j t", t=T)
                 if (q, c) in V_REGROUP:
                     nc.vector.tensor_copy(out=dst, in_=src)
                 else:

@@ -115,11 +115,12 @@ def tile_ternarylinear_kernel(tc, x, weight, grad_out, out):
 
         g_grp, g_codes, g_scales = {}, {}, {}
 
-        def regroup_g(q):
-            g_grp[q] = ggpool.tile([P, PASSES, CHUNK * PACK], BF16, tag="gg", name="g_grp_%d" % q, align_bytes=64)
+        def regroup_g(q, passes):
+            if q not in g_grp:
+                g_grp[q] = ggpool.tile([P, PASSES, CHUNK * PACK], BF16, tag="gg", name="g_grp_%d" % q, align_bytes=64)
             piece = [i for i, (a, b) in enumerate(G_PIECES) if a <= q * CHUNK < b][0]
             lo = q * CHUNK - G_PIECES[piece][0]
-            for c in range(PASSES):
+            for c in passes:
                 dst = g_grp[q][:, c, :].rearrange("k (t p j) -> k p j t", t=T, p=P)
                 src = g_raw[(piece, c)][:, :, lo : lo + CHUNK].rearrange("k j (p t) -> k p j t", t=T)
                 if (q, c) in V_REGROUP:
@@ -137,11 +138,9 @@ def tile_ternarylinear_kernel(tc, x, weight, grad_out, out):
             )
 
         quantise_x(0)
-        regroup_g(0)
+        regroup_g(0, (0, 1))
         quantise_x(1)
         quantise_g(0)
-        for q in range(1, LEAD):
-            regroup_g(q)
 
         for q in range(N_CHUNKS):
             ahead = q + LEAD
@@ -153,8 +152,10 @@ def tile_ternarylinear_kernel(tc, x, weight, grad_out, out):
             )
             for r in range(V_ABS_ROWS, T):
                 nc.scalar.activation(out=w_sb[q][:, r, :], in_=w_sb[q][:, r, :], func=ACT.Abs)
+            if q == 0:
+                regroup_g(1, (0,))
             if ahead < N_CHUNKS:
-                regroup_g(ahead)
+                regroup_g(ahead, (0, 1))
 
             o_sb = opool.tile([P, T, COLS], F32, tag="o", name="o_sb_%d" % q)
             for r in range(T):
@@ -182,8 +183,10 @@ def tile_ternarylinear_kernel(tc, x, weight, grad_out, out):
                         op0=ALU.is_le,
                         op1=ALU.mult,
                     )
-                if r == Q_AT and 0 < ahead - 1 < N_CHUNKS:
-                    quantise_g(ahead - 1)
+                if q == 0 and r == 2:
+                    regroup_g(1, (1,))
+                if q + 1 < N_CHUNKS and r == (3 if q == 0 else Q_AT):
+                    quantise_g(q + 1)
                 if q == N_CHUNKS - 1:
                     nc.sync.dma_start(out=o_view[q][:, r, :], in_=o_sb[:, r, :])
             if q < N_CHUNKS - 1:

@@ -28,7 +28,7 @@ FLOPS = 2 * TOKENS * COLS * ROWS
 
 G_PIECES = ((0, 512), (512, 2048), (2048, 4096))
 V_REGROUP = ((0, 1), (1, 1))
-V_ABS_ROWS = 2
+V_ABS_ROWS = 3
 LEAD = 2
 Q_AT = 1
 W_BUFS = 4

@@ -36,7 +36,7 @@ O_BUFS = 4
 GG_BUFS = 3
 GC_BUFS = 3
 W_EARLY = 3
-MANUAL = True
+MANUAL = False
 
 
 def tile_ternarylinear_kernel(tc, x, weight, grad_out, out):

from contextlib import ExitStack

import concourse.mybir as mybir

BF16 = mybir.dt.bfloat16
F32 = mybir.dt.float32
U32 = mybir.dt.uint32
U8 = mybir.dt.uint8
I32 = mybir.dt.int32
E4M3X4 = mybir.dt.float8_e4m3fn_x4
E5M2X4 = mybir.dt.float8_e5m2_x4
ALU = mybir.AluOpType
ACT = mybir.ActivationFunctionType

P = 128
PACK = 4
K_PASS = P * PACK
TOKENS, COLS, ROWS = 1024, 1024, 4096
PASSES = TOKENS // K_PASS
T = 4
CHUNK = P * T
N_CHUNKS = ROWS // CHUNK
N_TILE = 512
HALVES = COLS // N_TILE
CUT = 1.5

FLOPS = 2 * TOKENS * COLS * ROWS

G_PIECES = ((0, 512), (512, 2048), (2048, 4096))
V_REGROUP = ((0, 1), (1, 1))
V_ABS_ROWS = 3
LEAD = 2
Q_AT = 1
W_BUFS = 4
O_BUFS = 4
GG_BUFS = 3
GC_BUFS = 3
W_EARLY = 3
MANUAL = False


def tile_ternarylinear_kernel(tc, x, weight, grad_out, out):
    nc = tc.nc
    with ExitStack() as ctx:
        if MANUAL:
            ctx.enter_context(tc.manual_schedule())
        keep = ctx.enter_context(tc.tile_pool(name="keep", bufs=1))
        wpool = ctx.enter_context(tc.tile_pool(name="wpool", bufs=W_BUFS))
        opool = ctx.enter_context(tc.tile_pool(name="opool", bufs=O_BUFS))
        ggpool = ctx.enter_context(tc.tile_pool(name="ggpool", bufs=GG_BUFS))
        gcpool = ctx.enter_context(tc.tile_pool(name="gcpool", bufs=GC_BUFS))
        psum = ctx.enter_context(tc.psum_pool(name="psum", bufs=8))

        w_view = weight.rearrange("(q p t) k -> q p t k", p=P, t=T)
        o_view = out.rearrange("(q p t) k -> q p t k", p=P, t=T)

        x_raw = opool.tile([P, PASSES, PACK, COLS], BF16, tag="o", name="x_raw")
        for c in range(PASSES):
            nc.sync.dma_start(
                out=x_raw[:, c, :, :],
                in_=x[c * K_PASS : (c + 1) * K_PASS, :].rearrange("(p j) w -> p j w", j=PACK),
            )

        g_raw = {}

        def load_g(i):
            a, b = G_PIECES[i]
            for c in range(PASSES):
                g_raw[(i, c)] = keep.tile([P, PACK, b - a], BF16, name="g_raw_%d_%d" % (i, c))
                nc.sync.dma_start(
                    out=g_raw[(i, c)][:],
                    in_=grad_out[c * K_PASS : (c + 1) * K_PASS, a:b].rearrange("(p j) w -> p j w", j=PACK),
                )

        w_sb = {}

        def load_w(q):
            w_sb[q] = wpool.tile([P, T, COLS], BF16, tag="w", name="w_sb_%d" % q)
            nc.sync.dma_start(out=w_sb[q][:], in_=w_view[q])

        load_g(0)
        load_w(0)
        next_w = 1
        for i in range(1, len(G_PIECES)):
            load_g(i)
            if i == 1:
                while next_w < min(W_EARLY, W_BUFS):
                    load_w(next_w)
                    next_w += 1
        while next_w < W_BUFS:
            load_w(next_w)
            next_w += 1

        x_codes = keep.tile([P, PASSES, COLS], U32, name="x_codes", align_bytes=64)
        x_scales = keep.tile([P, PASSES, COLS], U8, name="x_scales", align_bytes=64)
        x_grp = {}
        half = COLS // 2
        for c in range(PASSES):
            x_grp[c] = ggpool.tile([P, COLS, PACK], BF16, tag="gg", name="x_grp_%d" % c, align_bytes=64)
            nc.vector.tensor_copy(
                out=x_grp[c][:, 0:half, :].rearrange("p (a i) j -> p a j i", i=4),
                in_=x_raw[:, c, :, 0:half].rearrange("p j (a i) -> p a j i", i=4),
            )
            nc.scalar.copy(
                out=x_grp[c][:, half:COLS, :].rearrange("p (a i) j -> p a j i", i=4),
                in_=x_raw[:, c, :, half:COLS].rearrange("p j (a i) -> p a j i", i=4),
            )

        def quantise_x(c):
            nc.vector.quantize_mx(
                out=x_codes[:, c, :].bitcast(E4M3X4),
                scales=x_scales[:, c, :],
                in_=x_grp[c][:].rearrange("p w j -> p (w j)"),
            )

        g_grp, g_codes, g_scales = {}, {}, {}

        def regroup_g(q, passes):
            if q not in g_grp:
                g_grp[q] = ggpool.tile([P, PASSES, CHUNK * PACK], BF16, tag="gg", name="g_grp_%d" % q, align_bytes=64)
            piece = [i for i, (a, b) in enumerate(G_PIECES) if a <= q * CHUNK < b][0]
            lo = q * CHUNK - G_PIECES[piece][0]
            for c in passes:
                dst = g_grp[q][:, c, :].rearrange("k (t p j) -> k p j t", t=T, p=P)
                src = g_raw[(piece, c)][:, :, lo : lo + CHUNK].rearrange("k j (p t) -> k p j t", t=T)
                if (q, c) in V_REGROUP:
                    nc.vector.tensor_copy(out=dst, in_=src)
                else:
                    nc.scalar.copy(out=dst, in_=src)

        def quantise_g(q):
            g_codes[q] = gcpool.tile([P, PASSES, CHUNK], U32, tag="gc", name="g_codes_%d" % q, align_bytes=64)
            g_scales[q] = gcpool.tile([P, PASSES, CHUNK], U8, tag="gs", name="g_scales_%d" % q, align_bytes=64)
            nc.vector.quantize_mx(
                out=g_codes[q][:].rearrange("p c w -> p (c w)").bitcast(E5M2X4),
                scales=g_scales[q][:].rearrange("p c w -> p (c w)"),
                in_=g_grp[q][:].rearrange("p c w -> p (c w)"),
            )

        quantise_x(0)
        regroup_g(0, (0, 1))
        quantise_x(1)
        quantise_g(0)

        for q in range(N_CHUNKS):
            ahead = q + LEAD
            nc.vector.tensor_single_scalar(
                out=w_sb[q][:, 0:V_ABS_ROWS, :].rearrange("p t k -> p (t k)").bitcast(I32),
                in_=w_sb[q][:, 0:V_ABS_ROWS, :].rearrange("p t k -> p (t k)").bitcast(I32),
                scalar=0x7FFF7FFF,
                op=ALU.bitwise_and,
            )
            for r in range(V_ABS_ROWS, T):
                nc.scalar.activation(out=w_sb[q][:, r, :], in_=w_sb[q][:, r, :], func=ACT.Abs)
            if q == 0:
                regroup_g(1, (0,))
            if ahead < N_CHUNKS:
                regroup_g(ahead, (0, 1))

            o_sb = opool.tile([P, T, COLS], F32, tag="o", name="o_sb_%d" % q)
            for r in range(T):
                acc = []
                for u in range(HALVES):
                    acc.append(psum.tile([P, N_TILE], F32, tag="acc", name="acc_%d_%d_%d" % (q, r, u)))
                for c in range(PASSES):
                    for u in range(HALVES):
                        nc.tensor.matmul_mx(
                            out=acc[u][:],
                            lhsT=g_codes[q][:, c, r * P : (r + 1) * P].bitcast(E5M2X4),
                            lhsT_scale=g_scales[q][:, c, r * P : (r + 1) * P],
                            rhs=x_codes[:, c, u * N_TILE : (u + 1) * N_TILE].bitcast(E4M3X4),
                            rhs_scale=x_scales[:, c, u * N_TILE : (u + 1) * N_TILE],
                            start=(c == 0),
                            stop=(c == PASSES - 1),
                        )
                for u in range(HALVES):
                    cols = slice(u * N_TILE, (u + 1) * N_TILE)
                    nc.vector.scalar_tensor_tensor(
                        out=o_sb[:, r, cols],
                        in0=w_sb[q][:, r, cols],
                        scalar=CUT,
                        in1=acc[u][:],
                        op0=ALU.is_le,
                        op1=ALU.mult,
                    )
                if q == 0 and r == 2:
                    regroup_g(1, (1,))
                if q + 1 < N_CHUNKS and r == (3 if q == 0 else Q_AT):
                    quantise_g(q + 1)
                if q == N_CHUNKS - 1:
                    nc.sync.dma_start(out=o_view[q][:, r, :], in_=o_sb[:, r, :])
            if q < N_CHUNKS - 1:
                nc.sync.dma_start(out=o_view[q], in_=o_sb[:])
            if next_w < N_CHUNKS:
                load_w(next_w)
                next_w += 1
